import numpy as np
import ml_dtypes


def mxq(x, axis, fmt="e4m3"):
    dtype, down = {"e4m3": (ml_dtypes.float8_e4m3fn, 7), "e5m2": (ml_dtypes.float8_e5m2, 14)}[fmt]
    v = np.moveaxis(np.asarray(x, np.float32).astype(ml_dtypes.bfloat16).astype(np.float64), axis, -1)
    blocks = v.reshape(v.shape[:-1] + (-1, 32))
    amax = np.abs(blocks).max(-1, keepdims=True)
    byte = np.maximum(np.where(amax > 0, np.frexp(amax)[1] - 1 + 127, 0) - down, 1)
    scale = np.exp2(byte - 127.0)
    codes = (blocks / scale).astype(np.float32).astype(dtype).astype(np.float64)
    return np.moveaxis((codes * scale).reshape(v.shape), -1, axis)


WIDE = False


def mx_kscale(k):
    if not WIDE:
        return np.ones(k)
    levels = np.array([10, -10, 5, -5, 0])
    a = np.random.permutation(np.resize(levels, k // 512 * 4)).reshape(k // 512, 4)
    idx = np.arange(k)
    return np.exp2(a[idx // 512, idx % 128 // 32])


BF16 = ml_dtypes.bfloat16


def bf(x):
    return np.asarray(x, np.float32).astype(BF16)


def f64(x):
    return np.asarray(x).astype(np.float64)


E2M1 = np.array([0.0, 0.5, 1.0, 1.5, 2.0, 3.0, 4.0, 6.0, -0.0, -0.5, -1.0, -1.5, -2.0, -3.0, -4.0, -6.0])


def pack_weight(w, fmt):
    k, n = w.shape
    w = f64(bf(w)).reshape(k // 32, 32, n)
    amax = np.abs(w).max(1)
    if fmt == "e4m3":
        byte = np.frexp(amax)[1] - 1 + 127 - 7
    else:
        mant, ex = np.frexp(amax / 6.0)
        byte = np.where(mant > 0.5, ex, ex - 1) + 127
    byte = np.clip(np.where(amax > 0, byte, 1), 1, 254)
    scaled = (w * np.exp2(127.0 - byte)[:, None, :]).reshape(k, n).astype(np.float32)
    by_word = np.ascontiguousarray(scaled.reshape(k // 512, 128, 4, n).transpose(0, 1, 3, 2))
    if fmt == "e4m3":
        words = by_word.astype(ml_dtypes.float8_e4m3fn).view(np.uint8)
    else:
        c = by_word.astype(ml_dtypes.float4_e2m1fn).view(np.uint8) & 0xF
        words = c[..., 0::2] | (c[..., 1::2] << 4)
    return np.ascontiguousarray(words), np.ascontiguousarray(byte.astype(np.uint8).reshape(k // 512, 16, n))


def unpack_weight(words, scales, fmt):
    g, p, n, _ = words.shape
    if fmt == "e4m3":
        vals = np.ascontiguousarray(words).view(ml_dtypes.float8_e4m3fn).astype(np.float64)
    else:
        nib = np.empty((g, p, n, 4), np.uint8)
        nib[..., 0::2] = words & 0xF
        nib[..., 1::2] = words >> 4
        vals = E2M1[nib]
    vals = vals * np.repeat(np.exp2(scales.astype(np.float64) - 127.0), 8, axis=1)[..., None]
    return vals.transpose(0, 1, 3, 2).reshape(g * 512, n)


B, D, G, S, K, E, H, C1, C2, C3 = 192, 1024, 16, 128, 128, 2, 512, 8, 64, 128
EPS = 1e-5


def sigmoid(v):
    return 1.0 / (1.0 + np.exp(-v))


def setup_inputs():
    t = mx_kscale(H)
    le = bf(np.maximum(np.random.standard_normal((B, G, S)), 0.0) * 1.25)
    ew1 = bf(np.random.standard_normal((E, H, S)) * 1.2 / np.sqrt(S))
    ew2 = np.random.standard_normal((E, K, H)) * 3.0 / np.sqrt(H) / t
    cat = np.ascontiguousarray(ew2.swapaxes(1, 2)).reshape(-1, K)
    ew2_words, ew2_scales = pack_weight(cat, "e4m3")
    return {"le": le,
            "ew1": ew1,
            "ew2_words": ew2_words,
            "ew2_scales": ew2_scales,
            "ebg": bf((1.0 + 0.1 * np.random.standard_normal((E, G, H))) * t),
            "ebb": bf(0.3 * np.random.standard_normal((E, G, H)) * t),
            "ebm": bf(0.3 * np.random.standard_normal((E, G, H))),
            "ebv": bf(0.5 + np.random.uniform(size=(E, G, H)))}


def reference(le, ew1, ew2_words, ew2_scales, ebg, ebb, ebm, ebv):
    u = (f64(le).reshape(B * G, S) @ f64(ew1).transpose(0, 2, 1)).reshape(E, B, G, H)
    gain = f64(ebg) / np.sqrt(f64(ebv) + EPS)
    h = np.maximum((u - f64(ebm)[:, None]) * gain[:, None] + f64(ebb)[:, None], 0.0)
    hq = mxq(h.reshape(E, B * G, H), 2, "e4m3")
    out = (hq @ unpack_weight(ew2_words, ew2_scales, "e4m3").reshape(E, H, K)).reshape(E, B, G, K)
    sel = sigmoid(out[0])
    sel = np.clip(1.2 * sel - 0.1, 0.0, 1.0)
    layer_bias = out[E - 1]
    return sel, layer_bias

@@ -1,0 +1,218 @@
+from contextlib import ExitStack
+
+import concourse.mybir as mybir
+from concourse.masks import make_identity
+
+F32 = mybir.dt.float32
+BF16 = mybir.dt.bfloat16
+I32 = mybir.dt.int32
+U32 = mybir.dt.uint32
+U8 = mybir.dt.uint8
+FP8X4 = mybir.dt.float8_e4m3fn_x4
+ACT = mybir.ActivationFunctionType
+ALU = mybir.AluOpType
+
+P = 128
+PACK = 4
+B, G, S, H, K, E = 192, 16, 128, 512, 128, 2
+EPS = 1e-5
+CHUNKS = G // 2
+REST = B - P
+TILES = 3
+COLS = TILES * P
+GCOLS = COLS // 2
+STEPS = CHUNKS * E
+LAG = 2
+RUN = 4
+FLOPS = 2 * B * G * S * E * H + 2 * B * G * H * E * K
+
+
+def tile_tgnetworkbias_pa_e_kernel(
+    tc, le, ew1, ew2_words, ew2_scales, ebg, ebb, ebm, ebv, out_0, out_1
+):
+    nc = tc.nc
+    with ExitStack() as ctx:
+        ctx.enter_context(tc.manual_schedule())
+        const = ctx.enter_context(tc.tile_pool(name="const", bufs=1))
+        work = ctx.enter_context(tc.tile_pool(name="work", bufs=3))
+        psum_u = ctx.enter_context(tc.psum_pool(name="psum_u", bufs=4))
+        psum_o = ctx.enter_context(tc.psum_pool(name="psum_o", bufs=2))
+
+        bn_rows = const.tile([P, H], BF16)
+        for i, table in enumerate((ebv, ebg, ebm, ebb)):
+            nc.sync.dma_start(
+                out=bn_rows[32 * i : 32 * i + 32, :], in_=table.rearrange("e g h -> (e g) h")
+            )
+        ew1_rows = const.tile([P, E, PACK, S], BF16)
+        nc.sync.dma_start(out=ew1_rows[:], in_=ew1.rearrange("e (p t) s -> p e t s", t=PACK))
+        le_rest = const.tile([P, CHUNKS, S], BF16)
+        for i in range(2):
+            nc.sync.dma_start(
+                out=le_rest[REST * i : REST * (i + 1)],
+                in_=le[P:B, CHUNKS * i : CHUNKS * (i + 1), :],
+            )
+        le_full = const.tile([P, G, S], BF16)
+        nc.sync.dma_start(out=le_full[:], in_=le[0:P])
+        w2_words = const.tile([P, E, PACK * K], U8, align_bytes=64)
+        w2_scales = const.tile([P, E, K], U8, align_bytes=64)
+        nc.vector.memset(w2_scales[:].bitcast(I32), 0)
+        nc.sync.dma_start(
+            out=w2_words[:].bitcast(I32),
+            in_=ew2_words.rearrange("e p n t -> p e (n t)").bitcast(I32),
+        )
+        for quad in range(4):
+            nc.sync.dma_start(
+                out=w2_scales[32 * quad : 32 * quad + 4].bitcast(I32),
+                in_=ew2_scales[:, 4 * quad : 4 * quad + 4, :].rearrange("e r n -> r e n").bitcast(I32),
+            )
+
+        ident = const.tile([P, P], BF16)
+        make_identity(nc, ident[:])
+        eps = const.tile([P, 1], F32)
+        nc.vector.memset(eps[:], EPS)
+        warm_sqrt = const.tile([P, 1], F32)
+        nc.scalar.activation(out=warm_sqrt[:], in_=eps[:], func=ACT.Sqrt)
+
+        bn_t = psum_o.tile([P, PACK, P], BF16, tag="o0")
+        for t in range(PACK):
+            nc.tensor.transpose(bn_t[:, t, :], bn_rows[:, t:H:PACK], ident[:])
+        std = const.tile([P, PACK, E * G], F32)
+        rstd = const.tile([P, PACK, E * G], F32)
+        gain = const.tile([P, PACK, E * G], F32)
+        mean_gain = const.tile([P, PACK, E * G], F32)
+        shift = const.tile([P, PACK, E * G], F32)
+        nc.scalar.activation(out=std[:], in_=bn_t[:, :, 0:32], func=ACT.Sqrt, bias=eps[:], scale=1.0)
+        warm_sigmoid = const.tile([P, 1], F32)
+        nc.scalar.activation(out=warm_sigmoid[:], in_=std[:, 0, 0:1], func=ACT.Sigmoid)
+        nc.vector.reciprocal(out=rstd[:], in_=std[:])
+        nc.vector.tensor_tensor(out=gain[:], in0=bn_t[:, :, 32:64], in1=rstd[:], op=ALU.mult)
+        nc.vector.tensor_tensor(out=mean_gain[:], in0=bn_t[:, :, 64:96], in1=gain[:], op=ALU.mult)
+        nc.vector.tensor_tensor(out=shift[:], in0=bn_t[:, :, 96:128], in1=mean_gain[:], op=ALU.subtract)
+
+        ew1_ps = psum_o.tile([P, E, PACK, P], BF16, tag="o1")
+        for e in range(E):
+            for t in range(PACK):
+                nc.tensor.transpose(ew1_ps[:, e, t, :], ew1_rows[:, e, t, :], ident[:])
+        ew1_t = const.tile([P, E, PACK, P], BF16)
+        nc.scalar.copy(out=ew1_t[:], in_=ew1_ps[:])
+
+        le_t = const.tile([P, CHUNKS, TILES, P], BF16)
+        for pair in range(CHUNKS // 2):
+            le_ps = psum_u.tile([P, 2, TILES, P], BF16, tag="u")
+            for c in range(2):
+                n = 2 * pair + c
+                nc.tensor.transpose(le_ps[:, c, 0, :], le_full[:, n, :], ident[:])
+                nc.tensor.transpose(le_ps[:, c, 1, :], le_rest[:, n, :], ident[:])
+                nc.tensor.transpose(le_ps[:, c, 2, :], le_full[:, n + CHUNKS, :], ident[:])
+            nc.vector.tensor_copy(out=le_t[:, 2 * pair : 2 * pair + 2], in_=le_ps[:])
+
+        planes_of = {}
+        words_of = {}
+        scales_of = {}
+        sums_of = {}
+        sel_of = {}
+
+        def hidden_layer(step):
+            n, e = divmod(step, E)
+            planes = work.tile([P, PACK, COLS], BF16, name="planes", tag="planes")
+            for t in range(PACK):
+                u = psum_u.tile([P, COLS], F32, name="u", tag="u")
+                nc.tensor.matmul(
+                    out=u[:],
+                    lhsT=ew1_t[:, e, t, :],
+                    rhs=le_t[:, n].rearrange("s j c -> s (j c)"),
+                    start=True,
+                    stop=True,
+                )
+                for i in range(2):
+                    row = G * e + n + CHUNKS * i
+                    cols = slice(GCOLS * i, GCOLS * (i + 1))
+                    nc.scalar.activation(
+                        out=planes[:, t, cols],
+                        in_=u[:, cols],
+                        func=ACT.Relu,
+                        bias=shift[:, t, row : row + 1],
+                        scale=gain[:, t, row : row + 1],
+                    )
+            planes_of[step] = planes
+
+        def regroup(step):
+            grouped = work.tile([P, COLS, PACK], BF16, name="grouped", tag="grouped", align_bytes=64)
+            nc.vector.tensor_copy(
+                out=grouped[:].rearrange("p (c i) t -> p c t i", i=RUN),
+                in_=planes_of[step][:].rearrange("p t (c i) -> p c t i", i=RUN),
+            )
+            return grouped
+
+        def quantise(step, grouped):
+            words = work.tile([P, COLS], U32, name="words", tag="words", align_bytes=64)
+            scales = work.tile([P, COLS], U8, name="scales", tag="scales", align_bytes=64)
+            for j in range(TILES):
+                cols = slice(P * j, P * (j + 1))
+                nc.vector.quantize_mx(
+                    out=words[:, cols].bitcast(FP8X4),
+                    scales=scales[:, cols],
+                    in_=grouped[:, cols, :].rearrange("p c t -> p (c t)"),
+                )
+            words_of[step] = words
+            scales_of[step] = scales
+
+        def second_matmul(step):
+            e = step % E
+            sums = psum_o.tile([P, TILES, K], F32, name="sums", tag="o%d" % e)
+            words = words_of[step]
+            scales = scales_of[step]
+            for j in range(TILES):
+                cols = slice(P * j, P * (j + 1))
+                nc.tensor.matmul_mx(
+                    out=sums[:, j, :],
+                    lhsT=words[:, cols].bitcast(FP8X4),
+                    lhsT_scale=scales[:, cols],
+                    rhs=w2_words[:, e, :].bitcast(FP8X4),
+                    rhs_scale=w2_scales[:, e, :],
+                    start=True,
+                    stop=True,
+                )
+            sums_of[step] = sums
+
+        def store(dst, result, n):
+            nc.sync.dma_start(out=dst[0:P, n:G:CHUNKS, :], in_=result[:, 0:TILES:2, :])
+            for i in range(2):
+                nc.sync.dma_start(
+                    out=dst[P:B, n + CHUNKS * i, :], in_=result[REST * i : REST * (i + 1), 1, :]
+                )
+
+        def sigmoid(step):
+            sel = work.tile([P, TILES, K], F32, name="sel", tag="sel")
+            nc.scalar.activation(out=sel[:], in_=sums_of[step][:], func=ACT.Sigmoid)
+            sel_of[step] = sel
+
+        def finish(step):
+            n, e = divmod(step, E)
+            if e == 0:
+                sel = sel_of[step]
+                nc.vector.tensor_scalar(
+                    out=sel[:], in0=sel[:], scalar1=1.2, scalar2=-0.1, op0=ALU.mult, op1=ALU.add
+                )
+                nc.vector.tensor_scalar(
+                    out=sel[:], in0=sel[:], scalar1=0.0, scalar2=1.0, op0=ALU.max, op1=ALU.min
+                )
+                store(out_0, sel, n)
+            else:
+                bias = work.tile([P, TILES, K], F32, name="bias", tag="bias")
+                nc.vector.tensor_copy(out=bias[:], in_=sums_of[step][:])
+                store(out_1, bias, n)
+
+        for r in range(STEPS + LAG):
+            if r < STEPS:
+                hidden_layer(r)
+            if r >= LAG:
+                second_matmul(r - LAG)
+                if (r - LAG) % E == 0:
+                    sigmoid(r - LAG)
+            if r < STEPS:
+                grouped = regroup(r)
+            if r >= LAG:
+                finish(r - LAG)
+            if r < STEPS:
+                quantise(r, grouped)

@@ -22,7 +22,7 @@ TILES = 3
 COLS = TILES * P
 GCOLS = COLS // 2
 STEPS = CHUNKS * E
-LAG = 2
+SCALAR_PLANES = 3
 RUN = 4
 FLOPS = 2 * B * G * S * E * H + 2 * B * G * H * E * K
 
@@ -36,7 +36,7 @@ def tile_tgnetworkbias_pa_e_kernel(
         const = ctx.enter_context(tc.tile_pool(name="const", bufs=1))
         work = ctx.enter_context(tc.tile_pool(name="work", bufs=3))
         psum_u = ctx.enter_context(tc.psum_pool(name="psum_u", bufs=4))
-        psum_o = ctx.enter_context(tc.psum_pool(name="psum_o", bufs=2))
+        psum_o = ctx.enter_context(tc.psum_pool(name="psum_o", bufs=4))
 
         bn_rows = const.tile([P, H], BF16)
         for i, table in enumerate((ebv, ebg, ebm, ebb)):
@@ -45,14 +45,20 @@ def tile_tgnetworkbias_pa_e_kernel(
             )
         ew1_rows = const.tile([P, E, PACK, S], BF16)
         nc.sync.dma_start(out=ew1_rows[:], in_=ew1.rearrange("e (p t) s -> p e t s", t=PACK))
+        le_full = const.tile([P, 2, CHUNKS, S], BF16)
         le_rest = const.tile([P, CHUNKS, S], BF16)
-        for i in range(2):
+        for half in range(2):
+            first = half * (CHUNKS // 2)
+            some = slice(first, first + CHUNKS // 2)
             nc.sync.dma_start(
-                out=le_rest[REST * i : REST * (i + 1)],
-                in_=le[P:B, CHUNKS * i : CHUNKS * (i + 1), :],
+                out=le_full[:, :, some, :],
+                in_=le[0:P].rearrange("b (i n) s -> b i n s", i=2)[:, :, some, :],
             )
-        le_full = const.tile([P, G, S], BF16)
-        nc.sync.dma_start(out=le_full[:], in_=le[0:P])
+            for i in range(2):
+                nc.sync.dma_start(
+                    out=le_rest[REST * i : REST * (i + 1), some, :],
+                    in_=le[P:B, CHUNKS * i + first : CHUNKS * i + first + CHUNKS // 2, :],
+                )
         w2_words = const.tile([P, E, PACK * K], U8, align_bytes=64)
         w2_scales = const.tile([P, E, K], U8, align_bytes=64)
         nc.vector.memset(w2_scales[:].bitcast(I32), 0)
@@ -73,38 +79,59 @@ def tile_tgnetworkbias_pa_e_kernel(
         warm_sqrt = const.tile([P, 1], F32)
         nc.scalar.activation(out=warm_sqrt[:], in_=eps[:], func=ACT.Sqrt)
 
-        bn_t = psum_o.tile([P, PACK, P], BF16, tag="o0")
+        bn_t = psum_o.tile([P, PACK, 4, E * G], BF16, tag="o")
         for t in range(PACK):
-            nc.tensor.transpose(bn_t[:, t, :], bn_rows[:, t:H:PACK], ident[:])
+            nc.tensor.transpose(
+                bn_t[:, t].rearrange("p i r -> p (i r)"), bn_rows[:, t:H:PACK], ident[:]
+            )
+        ew1_ps = psum_o.tile([P, E, PACK, P], BF16, tag="o")
+        for e in range(E):
+            for t in range(PACK):
+                nc.tensor.transpose(ew1_ps[:, e, t, :], ew1_rows[:, e, t, :], ident[:])
+        ew1_t = const.tile([P, E, PACK, P], BF16)
+
+        le_t = const.tile([P, CHUNKS, TILES, P], BF16)
+
+        def transpose_le(pair):
+            le_ps = psum_o.tile([P, 2, TILES, P], BF16, name="le_ps", tag="o")
+            for c in range(2):
+                n = 2 * pair + c
+                nc.tensor.transpose(le_ps[:, c, 0, :], le_full[:, 0, n, :], ident[:])
+                nc.tensor.transpose(le_ps[:, c, 1, :], le_rest[:, n, :], ident[:])
+                nc.tensor.transpose(le_ps[:, c, 2, :], le_full[:, 1, n, :], ident[:])
+            return le_ps
+
+        def keep_le(pair, le_ps):
+            nc.vector.tensor_copy(out=le_t[:, 2 * pair : 2 * pair + 2], in_=le_ps[:])
+
+        first_le = transpose_le(0)
+
         std = const.tile([P, PACK, E * G], F32)
         rstd = const.tile([P, PACK, E * G], F32)
         gain = const.tile([P, PACK, E * G], F32)
         mean_gain = const.tile([P, PACK, E * G], F32)
         shift = const.tile([P, PACK, E * G], F32)
-        nc.scalar.activation(out=std[:], in_=bn_t[:, :, 0:32], func=ACT.Sqrt, bias=eps[:], scale=1.0)
+        nc.scalar.activation(out=std[:], in_=bn_t[:, :, 0, :], func=ACT.Sqrt, bias=eps[:], scale=1.0)
         warm_sigmoid = const.tile([P, 1], F32)
         nc.scalar.activation(out=warm_sigmoid[:], in_=std[:, 0, 0:1], func=ACT.Sigmoid)
-        nc.vector.reciprocal(out=rstd[:], in_=std[:])
-        nc.vector.tensor_tensor(out=gain[:], in0=bn_t[:, :, 32:64], in1=rstd[:], op=ALU.mult)
-        nc.vector.tensor_tensor(out=mean_gain[:], in0=bn_t[:, :, 64:96], in1=gain[:], op=ALU.mult)
-        nc.vector.tensor_tensor(out=shift[:], in0=bn_t[:, :, 96:128], in1=mean_gain[:], op=ALU.subtract)
 
-        ew1_ps = psum_o.tile([P, E, PACK, P], BF16, tag="o1")
-        for e in range(E):
-            for t in range(PACK):
-                nc.tensor.transpose(ew1_ps[:, e, t, :], ew1_rows[:, e, t, :], ident[:])
-        ew1_t = const.tile([P, E, PACK, P], BF16)
-        nc.scalar.copy(out=ew1_t[:], in_=ew1_ps[:])
+        def prepare_expert(e):
+            rows = slice(G * e, G * (e + 1))
+            nc.vector.reciprocal(out=rstd[:, :, rows], in_=std[:, :, rows])
+            nc.vector.tensor_tensor(
+                out=gain[:, :, rows], in0=bn_t[:, :, 1, rows], in1=rstd[:, :, rows], op=ALU.mult
+            )
+            nc.vector.tensor_tensor(
+                out=mean_gain[:, :, rows], in0=bn_t[:, :, 2, rows], in1=gain[:, :, rows], op=ALU.mult
+            )
+            nc.vector.tensor_tensor(
+                out=shift[:, :, rows], in0=bn_t[:, :, 3, rows], in1=mean_gain[:, :, rows], op=ALU.subtract
+            )
+            nc.vector.tensor_copy(out=ew1_t[:, e], in_=ew1_ps[:, e])
 
-        le_t = const.tile([P, CHUNKS, TILES, P], BF16)
-        for pair in range(CHUNKS // 2):
-            le_ps = psum_u.tile([P, 2, TILES, P], BF16, tag="u")
-            for c in range(2):
-                n = 2 * pair + c
-                nc.tensor.transpose(le_ps[:, c, 0, :], le_full[:, n, :], ident[:])
-                nc.tensor.transpose(le_ps[:, c, 1, :], le_rest[:, n, :], ident[:])
-                nc.tensor.transpose(le_ps[:, c, 2, :], le_full[:, n + CHUNKS, :], ident[:])
-            nc.vector.tensor_copy(out=le_t[:, 2 * pair : 2 * pair + 2], in_=le_ps[:])
+        prepare_expert(0)
+        keep_le(0, first_le)
+        prepare_expert(1)
 
         planes_of = {}
         words_of = {}
@@ -127,20 +154,31 @@ def tile_tgnetworkbias_pa_e_kernel(
                 for i in range(2):
                     row = G * e + n + CHUNKS * i
                     cols = slice(GCOLS * i, GCOLS * (i + 1))
-                    nc.scalar.activation(
-                        out=planes[:, t, cols],
-                        in_=u[:, cols],
-                        func=ACT.Relu,
-                        bias=shift[:, t, row : row + 1],
-                        scale=gain[:, t, row : row + 1],
-                    )
+                    if t < SCALAR_PLANES:
+                        nc.scalar.activation(
+                            out=planes[:, t, cols],
+                            in_=u[:, cols],
+                            func=ACT.Identity,
+                            bias=shift[:, t, row : row + 1],
+                            scale=gain[:, t, row : row + 1],
+                        )
+                    else:
+                        nc.vector.tensor_scalar(
+                            out=planes[:, t, cols],
+                            in0=u[:, cols],
+                            scalar1=gain[:, t, row : row + 1],
+                            scalar2=shift[:, t, row : row + 1],
+                            op0=ALU.mult,
+                            op1=ALU.add,
+                        )
             planes_of[step] = planes
 
         def regroup(step):
             grouped = work.tile([P, COLS, PACK], BF16, name="grouped", tag="grouped", align_bytes=64)
-            nc.vector.tensor_copy(
+            nc.vector.tensor_scalar_max(
                 out=grouped[:].rearrange("p (c i) t -> p c t i", i=RUN),
-                in_=planes_of[step][:].rearrange("p t (c i) -> p c t i", i=RUN),
+                in0=planes_of[step][:].rearrange("p t (c i) -> p c t i", i=RUN),
+                scalar1=0.0,
             )
             return grouped
 
@@ -159,15 +197,13 @@ def tile_tgnetworkbias_pa_e_kernel(
 
         def second_matmul(step):
             e = step % E
-            sums = psum_o.tile([P, TILES, K], F32, name="sums", tag="o%d" % e)
-            words = words_of[step]
-            scales = scales_of[step]
+            sums = psum_o.tile([P, TILES, K], F32, name="sums", tag="o")
             for j in range(TILES):
                 cols = slice(P * j, P * (j + 1))
                 nc.tensor.matmul_mx(
                     out=sums[:, j, :],
-                    lhsT=words[:, cols].bitcast(FP8X4),
-                    lhsT_scale=scales[:, cols],
+                    lhsT=words_of[step][:, cols].bitcast(FP8X4),
+                    lhsT_scale=scales_of[step][:, cols],
                     rhs=w2_words[:, e, :].bitcast(FP8X4),
                     rhs_scale=w2_scales[:, e, :],
                     start=True,
@@ -182,12 +218,18 @@ def tile_tgnetworkbias_pa_e_kernel(
                     out=dst[P:B, n + CHUNKS * i, :], in_=result[REST * i : REST * (i + 1), 1, :]
                 )
 
-        def sigmoid(step):
-            sel = work.tile([P, TILES, K], F32, name="sel", tag="sel")
-            nc.scalar.activation(out=sel[:], in_=sums_of[step][:], func=ACT.Sigmoid)
-            sel_of[step] = sel
+        def leave_psum(step):
+            n, e = divmod(step, E)
+            if e == 0:
+                sel = work.tile([P, TILES, K], F32, name="sel", tag="sel")
+                nc.scalar.activation(out=sel[:], in_=sums_of[step][:], func=ACT.Sigmoid)
+                sel_of[step] = sel
+            else:
+                layer_bias = work.tile([P, TILES, K], F32, name="layer_bias", tag="layer_bias")
+                nc.scalar.copy(out=layer_bias[:], in_=sums_of[step][:])
+                store(out_1, layer_bias, n)
 
-        def finish(step):
+        def stretch_and_clip(step):
             n, e = divmod(step, E)
             if e == 0:
                 sel = sel_of[step]
@@ -198,21 +240,21 @@ def tile_tgnetworkbias_pa_e_kernel(
                     out=sel[:], in0=sel[:], scalar1=0.0, scalar2=1.0, op0=ALU.max, op1=ALU.min
                 )
                 store(out_0, sel, n)
-            else:
-                bias = work.tile([P, TILES, K], F32, name="bias", tag="bias")
-                nc.vector.tensor_copy(out=bias[:], in_=sums_of[step][:])
-                store(out_1, bias, n)
 
-        for r in range(STEPS + LAG):
-            if r < STEPS:
+        def live(step):
+            return 0 <= step < STEPS
+
+        for r in range(STEPS + 3):
+            if live(r - 1):
+                grouped = regroup(r - 1)
+            if live(r):
                 hidden_layer(r)
-            if r >= LAG:
-                second_matmul(r - LAG)
-                if (r - LAG) % E == 0:
-                    sigmoid(r - LAG)
-            if r < STEPS:
-                grouped = regroup(r)
-            if r >= LAG:
-                finish(r - LAG)
-            if r < STEPS:
-                quantise(r, grouped)
+            if r + 1 < CHUNKS // 2:
+                keep_le(r + 1, transpose_le(r + 1))
+            if live(r - 2):
+                second_matmul(r - 2)
+                leave_psum(r - 2)
+            if live(r - 3):
+                stretch_and_clip(r - 3)
+            if live(r - 1):
+                quantise(r - 1, grouped)

@@ -84,11 +84,14 @@ def tile_tgnetworkbias_pa_e_kernel(
             nc.tensor.transpose(
                 bn_t[:, t].rearrange("p i r -> p (i r)"), bn_rows[:, t:H:PACK], ident[:]
             )
-        ew1_ps = psum_o.tile([P, E, PACK, P], BF16, tag="o")
-        for e in range(E):
-            for t in range(PACK):
-                nc.tensor.transpose(ew1_ps[:, e, t, :], ew1_rows[:, e, t, :], ident[:])
+
         ew1_t = const.tile([P, E, PACK, P], BF16)
+
+        def transpose_ew1(e):
+            ew1_ps = psum_o.tile([P, PACK, P], BF16, name="ew1_ps", tag="o")
+            for t in range(PACK):
+                nc.tensor.transpose(ew1_ps[:, t, :], ew1_rows[:, e, t, :], ident[:])
+            return ew1_ps
 
         le_t = const.tile([P, CHUNKS, TILES, P], BF16)
 
@@ -104,7 +107,9 @@ def tile_tgnetworkbias_pa_e_kernel(
         def keep_le(pair, le_ps):
             nc.vector.tensor_copy(out=le_t[:, 2 * pair : 2 * pair + 2], in_=le_ps[:])
 
-        first_le = transpose_le(0)
+        ew1_ps_of = {0: transpose_ew1(0)}
+        le_ps_of = {0: transpose_le(0)}
+        ew1_ps_of[1] = transpose_ew1(1)
 
         std = const.tile([P, PACK, E * G], F32)
         rstd = const.tile([P, PACK, E * G], F32)
@@ -115,9 +120,12 @@ def tile_tgnetworkbias_pa_e_kernel(
         warm_sigmoid = const.tile([P, 1], F32)
         nc.scalar.activation(out=warm_sigmoid[:], in_=std[:, 0, 0:1], func=ACT.Sigmoid)
 
-        def prepare_expert(e):
+        def invert_std(e):
             rows = slice(G * e, G * (e + 1))
             nc.vector.reciprocal(out=rstd[:, :, rows], in_=std[:, :, rows])
+
+        def gain_and_shift(e):
+            rows = slice(G * e, G * (e + 1))
             nc.vector.tensor_tensor(
                 out=gain[:, :, rows], in0=bn_t[:, :, 1, rows], in1=rstd[:, :, rows], op=ALU.mult
             )
@@ -127,11 +135,17 @@ def tile_tgnetworkbias_pa_e_kernel(
             nc.vector.tensor_tensor(
                 out=shift[:, :, rows], in0=bn_t[:, :, 3, rows], in1=mean_gain[:, :, rows], op=ALU.subtract
             )
-            nc.vector.tensor_copy(out=ew1_t[:, e], in_=ew1_ps[:, e])
 
-        prepare_expert(0)
-        keep_le(0, first_le)
-        prepare_expert(1)
+        def keep_ew1(e):
+            nc.vector.tensor_copy(out=ew1_t[:, e], in_=ew1_ps_of[e][:])
+
+        invert_std(0)
+        keep_ew1(0)
+        keep_le(0, le_ps_of[0])
+        gain_and_shift(0)
+        invert_std(1)
+        gain_and_shift(1)
+        keep_ew1(1)
 
         planes_of = {}
         words_of = {}
@@ -229,13 +243,17 @@ def tile_tgnetworkbias_pa_e_kernel(
                 nc.scalar.copy(out=layer_bias[:], in_=sums_of[step][:])
                 store(out_1, layer_bias, n)
 
-        def stretch_and_clip(step):
-            n, e = divmod(step, E)
-            if e == 0:
+        def stretch(step):
+            if step % E == 0:
                 sel = sel_of[step]
                 nc.vector.tensor_scalar(
                     out=sel[:], in0=sel[:], scalar1=1.2, scalar2=-0.1, op0=ALU.mult, op1=ALU.add
                 )
+
+        def clip(step):
+            n, e = divmod(step, E)
+            if e == 0:
+                sel = sel_of[step]
                 nc.vector.tensor_scalar(
                     out=sel[:], in0=sel[:], scalar1=0.0, scalar2=1.0, op0=ALU.max, op1=ALU.min
                 )
@@ -247,14 +265,18 @@ def tile_tgnetworkbias_pa_e_kernel(
         for r in range(STEPS + 3):
             if live(r - 1):
                 grouped = regroup(r - 1)
+            if live(r - 3):
+                stretch(r - 3)
             if live(r):
                 hidden_layer(r)
             if r + 1 < CHUNKS // 2:
-                keep_le(r + 1, transpose_le(r + 1))
+                le_ps_of[r + 1] = transpose_le(r + 1)
             if live(r - 2):
                 second_matmul(r - 2)
                 leave_psum(r - 2)
             if live(r - 3):
-                stretch_and_clip(r - 3)
+                clip(r - 3)
             if live(r - 1):
                 quantise(r - 1, grouped)
+            if 1 <= r < CHUNKS // 2:
+                keep_le(r, le_ps_of[r])

@@ -22,9 +22,16 @@ TILES = 3
 COLS = TILES * P
 GCOLS = COLS // 2
 STEPS = CHUNKS * E
-SCALAR_PLANES = 3
 RUN = 4
 FLOPS = 2 * B * G * S * E * H + 2 * B * G * H * E * K
+
+
+def vector_planes(step):
+    if step == 0:
+        return 2
+    if step >= STEPS - 2 or step % 4 == 3:
+        return 0
+    return 1
 
 
 def tile_tgnetworkbias_pa_e_kernel(
@@ -43,13 +50,11 @@ def tile_tgnetworkbias_pa_e_kernel(
             nc.sync.dma_start(
                 out=bn_rows[32 * i : 32 * i + 32, :], in_=table.rearrange("e g h -> (e g) h")
             )
-        ew1_rows = const.tile([P, E, PACK, S], BF16)
-        nc.sync.dma_start(out=ew1_rows[:], in_=ew1.rearrange("e (p t) s -> p e t s", t=PACK))
         le_full = const.tile([P, 2, CHUNKS, S], BF16)
         le_rest = const.tile([P, CHUNKS, S], BF16)
-        for half in range(2):
-            first = half * (CHUNKS // 2)
-            some = slice(first, first + CHUNKS // 2)
+
+        def load_le(first, count):
+            some = slice(first, first + count)
             nc.sync.dma_start(
                 out=le_full[:, :, some, :],
                 in_=le[0:P].rearrange("b (i n) s -> b i n s", i=2)[:, :, some, :],
@@ -57,8 +62,21 @@ def tile_tgnetworkbias_pa_e_kernel(
             for i in range(2):
                 nc.sync.dma_start(
                     out=le_rest[REST * i : REST * (i + 1), some, :],
-                    in_=le[P:B, CHUNKS * i + first : CHUNKS * i + first + CHUNKS // 2, :],
+                    in_=le[P:B, CHUNKS * i + first : CHUNKS * i + first + count, :],
                 )
+
+        ew1_rows = const.tile([P, E, PACK, S], BF16)
+
+        def load_ew1(e):
+            nc.sync.dma_start(
+                out=ew1_rows[:, e], in_=ew1[e].rearrange("(p t) s -> p t s", t=PACK)
+            )
+
+        load_le(0, 2)
+        load_ew1(0)
+        load_ew1(1)
+        load_le(2, 2)
+        load_le(4, 4)
         w2_words = const.tile([P, E, PACK * K], U8, align_bytes=64)
         w2_scales = const.tile([P, E, K], U8, align_bytes=64)
         nc.vector.memset(w2_scales[:].bitcast(I32), 0)
@@ -104,13 +122,6 @@ def tile_tgnetworkbias_pa_e_kernel(
                 nc.tensor.transpose(le_ps[:, c, 2, :], le_full[:, 1, n, :], ident[:])
             return le_ps
 
-        def keep_le(pair, le_ps):
-            nc.vector.tensor_copy(out=le_t[:, 2 * pair : 2 * pair + 2], in_=le_ps[:])
-
-        ew1_ps_of = {0: transpose_ew1(0)}
-        le_ps_of = {0: transpose_le(0)}
-        ew1_ps_of[1] = transpose_ew1(1)
-
         std = const.tile([P, PACK, E * G], F32)
         rstd = const.tile([P, PACK, E * G], F32)
         gain = const.tile([P, PACK, E * G], F32)
@@ -120,32 +131,17 @@ def tile_tgnetworkbias_pa_e_kernel(
         warm_sigmoid = const.tile([P, 1], F32)
         nc.scalar.activation(out=warm_sigmoid[:], in_=std[:, 0, 0:1], func=ACT.Sigmoid)
 
-        def invert_std(e):
-            rows = slice(G * e, G * (e + 1))
-            nc.vector.reciprocal(out=rstd[:, :, rows], in_=std[:, :, rows])
+        le_ps_of = {0: transpose_le(0)}
+        ew1_ps_of = {0: transpose_ew1(0), 1: transpose_ew1(1)}
 
-        def gain_and_shift(e):
-            rows = slice(G * e, G * (e + 1))
-            nc.vector.tensor_tensor(
-                out=gain[:, :, rows], in0=bn_t[:, :, 1, rows], in1=rstd[:, :, rows], op=ALU.mult
-            )
-            nc.vector.tensor_tensor(
-                out=mean_gain[:, :, rows], in0=bn_t[:, :, 2, rows], in1=gain[:, :, rows], op=ALU.mult
-            )
-            nc.vector.tensor_tensor(
-                out=shift[:, :, rows], in0=bn_t[:, :, 3, rows], in1=mean_gain[:, :, rows], op=ALU.subtract
-            )
-
-        def keep_ew1(e):
-            nc.vector.tensor_copy(out=ew1_t[:, e], in_=ew1_ps_of[e][:])
-
-        invert_std(0)
-        keep_ew1(0)
-        keep_le(0, le_ps_of[0])
-        gain_and_shift(0)
-        invert_std(1)
-        gain_and_shift(1)
-        keep_ew1(1)
+        nc.vector.reciprocal(out=rstd[:], in_=std[:])
+        nc.vector.tensor_copy(out=le_t[:, 0], in_=le_ps_of[0][:, 0])
+        nc.vector.tensor_tensor(out=gain[:], in0=bn_t[:, :, 1, :], in1=rstd[:], op=ALU.mult)
+        nc.vector.tensor_copy(out=ew1_t[:, 0], in_=ew1_ps_of[0][:])
+        nc.vector.tensor_tensor(out=mean_gain[:], in0=bn_t[:, :, 2, :], in1=gain[:], op=ALU.mult)
+        nc.vector.tensor_copy(out=ew1_t[:, 1], in_=ew1_ps_of[1][:])
+        nc.vector.tensor_tensor(out=shift[:], in0=bn_t[:, :, 3, :], in1=mean_gain[:], op=ALU.subtract)
+        nc.vector.tensor_copy(out=le_t[:, 1], in_=le_ps_of[0][:, 1])
 
         planes_of = {}
         words_of = {}
@@ -168,7 +164,7 @@ def tile_tgnetworkbias_pa_e_kernel(
                 for i in range(2):
                     row = G * e + n + CHUNKS * i
                     cols = slice(GCOLS * i, GCOLS * (i + 1))
-                    if t < SCALAR_PLANES:
+                    if t < PACK - vector_planes(step):
                         nc.scalar.activation(
                             out=planes[:, t, cols],
                             in_=u[:, cols],
@@ -199,8 +195,7 @@ def tile_tgnetworkbias_pa_e_kernel(
         def quantise(step, grouped):
             words = work.tile([P, COLS], U32, name="words", tag="words", align_bytes=64)
             scales = work.tile([P, COLS], U8, name="scales", tag="scales", align_bytes=64)
-            for j in range(TILES):
-                cols = slice(P * j, P * (j + 1))
+            for cols in (slice(0, 2 * P), slice(2 * P, COLS)):
                 nc.vector.quantize_mx(
                     out=words[:, cols].bitcast(FP8X4),
                     scales=scales[:, cols],
@@ -271,6 +266,7 @@ def tile_tgnetworkbias_pa_e_kernel(
                 hidden_layer(r)
             if r + 1 < CHUNKS // 2:
                 le_ps_of[r + 1] = transpose_le(r + 1)
+                nc.scalar.copy(out=le_t[:, 2 * r + 2 : 2 * r + 4], in_=le_ps_of[r + 1][:])
             if live(r - 2):
                 second_matmul(r - 2)
                 leave_psum(r - 2)
@@ -278,5 +274,3 @@ def tile_tgnetworkbias_pa_e_kernel(
                 clip(r - 3)
             if live(r - 1):
                 quantise(r - 1, grouped)
-            if 1 <= r < CHUNKS // 2:
-                keep_le(r, le_ps_of[r])

@@ -149,68 +149,83 @@ def tile_tgnetworkbias_pa_e_kernel(
         sums_of = {}
         sel_of = {}
 
-        def hidden_layer(step):
+        u_of = {}
+        grouped_of = {}
+
+        def first_matmul(step, t):
             n, e = divmod(step, E)
-            planes = work.tile([P, PACK, COLS], BF16, name="planes", tag="planes")
-            for t in range(PACK):
-                u = psum_u.tile([P, COLS], F32, name="u", tag="u")
-                nc.tensor.matmul(
-                    out=u[:],
-                    lhsT=ew1_t[:, e, t, :],
-                    rhs=le_t[:, n].rearrange("s j c -> s (j c)"),
-                    start=True,
-                    stop=True,
+            u = psum_u.tile([P, COLS], F32, name="u", tag="u")
+            nc.tensor.matmul(
+                out=u[:],
+                lhsT=ew1_t[:, e, t, :],
+                rhs=le_t[:, n].rearrange("s j c -> s (j c)"),
+                start=True,
+                stop=True,
+            )
+            u_of[step, t] = u
+
+        def batch_norm(step, t, i):
+            n, e = divmod(step, E)
+            row = G * e + n + CHUNKS * i
+            cols = slice(GCOLS * i, GCOLS * (i + 1))
+            if t < PACK - vector_planes(step):
+                nc.scalar.activation(
+                    out=planes_of[step][:, t, cols],
+                    in_=u_of[step, t][:, cols],
+                    func=ACT.Identity,
+                    bias=shift[:, t, row : row + 1],
+                    scale=gain[:, t, row : row + 1],
                 )
-                for i in range(2):
-                    row = G * e + n + CHUNKS * i
-                    cols = slice(GCOLS * i, GCOLS * (i + 1))
-                    if t < PACK - vector_planes(step):
-                        nc.scalar.activation(
-                            out=planes[:, t, cols],
-                            in_=u[:, cols],
-                            func=ACT.Identity,
-                            bias=shift[:, t, row : row + 1],
-                            scale=gain[:, t, row : row + 1],
-                        )
-                    else:
-                        nc.vector.tensor_scalar(
-                            out=planes[:, t, cols],
-                            in0=u[:, cols],
-                            scalar1=gain[:, t, row : row + 1],
-                            scalar2=shift[:, t, row : row + 1],
-                            op0=ALU.mult,
-                            op1=ALU.add,
-                        )
+            else:
+                nc.vector.tensor_scalar(
+                    out=planes_of[step][:, t, cols],
+                    in0=u_of[step, t][:, cols],
+                    scalar1=gain[:, t, row : row + 1],
+                    scalar2=shift[:, t, row : row + 1],
+                    op0=ALU.mult,
+                    op1=ALU.add,
+                )
+
+        def new_planes(step):
+            planes = work.tile([P, PACK, COLS], BF16, name="planes", tag="planes")
             planes_of[step] = planes
 
-        def regroup(step):
-            grouped = work.tile([P, COLS, PACK], BF16, name="grouped", tag="grouped", align_bytes=64)
+        def hidden_layer(step):
+            new_planes(step)
+            for t in range(PACK):
+                first_matmul(step, t)
+                for i in range(2):
+                    batch_norm(step, t, i)
+
+        def regroup(step, cols):
+            if step not in grouped_of:
+                grouped = work.tile([P, COLS, PACK], BF16, name="grouped", tag="grouped", align_bytes=64)
+                grouped_of[step] = grouped
             nc.vector.tensor_scalar_max(
-                out=grouped[:].rearrange("p (c i) t -> p c t i", i=RUN),
-                in0=planes_of[step][:].rearrange("p t (c i) -> p c t i", i=RUN),
+                out=grouped_of[step][:, cols, :].rearrange("p (c i) t -> p c t i", i=RUN),
+                in0=planes_of[step][:, :, cols].rearrange("p t (c i) -> p c t i", i=RUN),
                 scalar1=0.0,
             )
-            return grouped
 
-        def quantise(step, grouped):
-            words = work.tile([P, COLS], U32, name="words", tag="words", align_bytes=64)
-            scales = work.tile([P, COLS], U8, name="scales", tag="scales", align_bytes=64)
-            for cols in (slice(0, 2 * P), slice(2 * P, COLS)):
-                nc.vector.quantize_mx(
-                    out=words[:, cols].bitcast(FP8X4),
-                    scales=scales[:, cols],
-                    in_=grouped[:, cols, :].rearrange("p c t -> p (c t)"),
-                )
-            words_of[step] = words
-            scales_of[step] = scales
+        def quantise(step, cols):
+            if step not in words_of:
+                words = work.tile([P, COLS], U32, name="words", tag="words", align_bytes=64)
+                scales = work.tile([P, COLS], U8, name="scales", tag="scales", align_bytes=64)
+                words_of[step] = words
+                scales_of[step] = scales
+            nc.vector.quantize_mx(
+                out=words_of[step][:, cols].bitcast(FP8X4),
+                scales=scales_of[step][:, cols],
+                in_=grouped_of[step][:, cols, :].rearrange("p c t -> p (c t)"),
+            )
 
-        def second_matmul(step):
+        def second_matmul(step, tiles):
             e = step % E
-            sums = psum_o.tile([P, TILES, K], F32, name="sums", tag="o")
-            for j in range(TILES):
+            sums = psum_o.tile([P, len(tiles), K], F32, name="sums", tag="o")
+            for place, j in enumerate(tiles):
                 cols = slice(P * j, P * (j + 1))
                 nc.tensor.matmul_mx(
-                    out=sums[:, j, :],
+                    out=sums[:, place, :],
                     lhsT=words_of[step][:, cols].bitcast(FP8X4),
                     lhsT_scale=scales_of[step][:, cols],
                     rhs=w2_words[:, e, :].bitcast(FP8X4),
@@ -257,20 +272,60 @@ def tile_tgnetworkbias_pa_e_kernel(
         def live(step):
             return 0 <= step < STEPS
 
-        for r in range(STEPS + 3):
+        ALL = slice(0, COLS)
+        TWO_TILES = slice(0, 2 * P)
+        THIRD_TILE = slice(2 * P, COLS)
+        LAST = STEPS - 1
+
+        for r in range(LAST):
             if live(r - 1):
-                grouped = regroup(r - 1)
+                regroup(r - 1, ALL)
             if live(r - 3):
                 stretch(r - 3)
-            if live(r):
-                hidden_layer(r)
+            if live(r - 4):
+                clip(r - 4)
+            hidden_layer(r)
             if r + 1 < CHUNKS // 2:
                 le_ps_of[r + 1] = transpose_le(r + 1)
                 nc.scalar.copy(out=le_t[:, 2 * r + 2 : 2 * r + 4], in_=le_ps_of[r + 1][:])
             if live(r - 2):
-                second_matmul(r - 2)
+                second_matmul(r - 2, range(TILES))
                 leave_psum(r - 2)
-            if live(r - 3):
-                clip(r - 3)
             if live(r - 1):
-                quantise(r - 1, grouped)
+                quantise(r - 1, TWO_TILES)
+                quantise(r - 1, THIRD_TILE)
+
+        regroup(LAST - 1, ALL)
+        stretch(LAST - 3)
+        new_planes(LAST)
+        for t in range(PACK):
+            first_matmul(LAST, t)
+        for t in range(PACK):
+            batch_norm(LAST, t, 0)
+        second_matmul(LAST - 2, range(TILES))
+        quantise(LAST - 1, TWO_TILES)
+        quantise(LAST - 1, THIRD_TILE)
+        for t in range(PACK):
+            batch_norm(LAST, t, 1)
+        regroup(LAST, slice(0, GCOLS))
+        clip(LAST - 3)
+        leave_psum(LAST - 2)
+        regroup(LAST, slice(GCOLS, COLS))
+        second_matmul(LAST - 1, range(TILES))
+        leave_psum(LAST - 1)
+        quantise(LAST, slice(0, P))
+        quantise(LAST, slice(P, COLS))
+        n_last = LAST // E
+        layer_bias = work.tile([P, TILES, K], F32, name="layer_bias", tag="layer_bias")
+        second_matmul(LAST, [0])
+        nc.scalar.copy(out=layer_bias[:, 0:1, :], in_=sums_of[LAST][:])
+        nc.sync.dma_start(out=out_1[0:P, n_last, :], in_=layer_bias[:, 0, :])
+        second_matmul(LAST, [1, 2])
+        stretch(LAST - 1)
+        nc.scalar.copy(out=layer_bias[:, 1:TILES, :], in_=sums_of[LAST][:])
+        nc.sync.dma_start(out=out_1[0:P, n_last + CHUNKS, :], in_=layer_bias[:, 2, :])
+        for i in range(2):
+            nc.sync.dma_start(
+                out=out_1[P:B, n_last + CHUNKS * i, :], in_=layer_bias[REST * i : REST * (i + 1), 1, :]
+            )
+        clip(LAST - 1)

@@ -22,6 +22,8 @@ TILES = 3
 COLS = TILES * P
 GCOLS = COLS // 2
 STEPS = CHUNKS * E
+WARM_COLS = 512
+WARM_PASSES = 4
 RUN = 4
 FLOPS = 2 * B * G * S * E * H + 2 * B * G * H * E * K
 
@@ -44,6 +46,12 @@ def tile_tgnetworkbias_pa_e_kernel(
         work = ctx.enter_context(tc.tile_pool(name="work", bufs=3))
         psum_u = ctx.enter_context(tc.psum_pool(name="psum_u", bufs=4))
         psum_o = ctx.enter_context(tc.psum_pool(name="psum_o", bufs=4))
+
+        zeros = const.tile([P, WARM_COLS], BF16)
+        nc.vector.memset(zeros[:], 0.0)
+        warm = psum_u.tile([P, WARM_COLS], F32, name="warm", tag="u")
+        for spare in range(WARM_PASSES):
+            nc.tensor.matmul(out=warm[:], lhsT=zeros[:, 0:P], rhs=zeros[:], start=True, stop=True)
 
         bn_rows = const.tile([P, H], BF16)
         for i, table in enumerate((ebv, ebg, ebm, ebb)):

from contextlib import ExitStack

import concourse.mybir as mybir
from concourse.masks import make_identity

F32 = mybir.dt.float32
BF16 = mybir.dt.bfloat16
I32 = mybir.dt.int32
U32 = mybir.dt.uint32
U8 = mybir.dt.uint8
FP8X4 = mybir.dt.float8_e4m3fn_x4
ACT = mybir.ActivationFunctionType
ALU = mybir.AluOpType

P = 128
PACK = 4
B, G, S, H, K, E = 192, 16, 128, 512, 128, 2
EPS = 1e-5
CHUNKS = G // 2
REST = B - P
TILES = 3
COLS = TILES * P
GCOLS = COLS // 2
STEPS = CHUNKS * E
WARM_COLS = 512
WARM_PASSES = 4
RUN = 4
FLOPS = 2 * B * G * S * E * H + 2 * B * G * H * E * K


def vector_planes(step):
    if step == 0:
        return 2
    if step >= STEPS - 2 or step % 4 == 3:
        return 0
    return 1


def tile_tgnetworkbias_pa_e_kernel(
    tc, le, ew1, ew2_words, ew2_scales, ebg, ebb, ebm, ebv, out_0, out_1
):
    nc = tc.nc
    with ExitStack() as ctx:
        ctx.enter_context(tc.manual_schedule())
        const = ctx.enter_context(tc.tile_pool(name="const", bufs=1))
        work = ctx.enter_context(tc.tile_pool(name="work", bufs=3))
        psum_u = ctx.enter_context(tc.psum_pool(name="psum_u", bufs=4))
        psum_o = ctx.enter_context(tc.psum_pool(name="psum_o", bufs=4))

        zeros = const.tile([P, WARM_COLS], BF16)
        nc.vector.memset(zeros[:], 0.0)
        warm = psum_u.tile([P, WARM_COLS], F32, name="warm", tag="u")
        for spare in range(WARM_PASSES):
            nc.tensor.matmul(out=warm[:], lhsT=zeros[:, 0:P], rhs=zeros[:], start=True, stop=True)

        bn_rows = const.tile([P, H], BF16)
        for i, table in enumerate((ebv, ebg, ebm, ebb)):
            nc.sync.dma_start(
                out=bn_rows[32 * i : 32 * i + 32, :], in_=table.rearrange("e g h -> (e g) h")
            )
        le_full = const.tile([P, 2, CHUNKS, S], BF16)
        le_rest = const.tile([P, CHUNKS, S], BF16)

        def load_le(first, count):
            some = slice(first, first + count)
            nc.sync.dma_start(
                out=le_full[:, :, some, :],
                in_=le[0:P].rearrange("b (i n) s -> b i n s", i=2)[:, :, some, :],
            )
            for i in range(2):
                nc.sync.dma_start(
                    out=le_rest[REST * i : REST * (i + 1), some, :],
                    in_=le[P:B, CHUNKS * i + first : CHUNKS * i + first + count, :],
                )

        ew1_rows = const.tile([P, E, PACK, S], BF16)

        def load_ew1(e):
            nc.sync.dma_start(
                out=ew1_rows[:, e], in_=ew1[e].rearrange("(p t) s -> p t s", t=PACK)
            )

        load_le(0, 2)
        load_ew1(0)
        load_ew1(1)
        load_le(2, 2)
        load_le(4, 4)
        w2_words = const.tile([P, E, PACK * K], U8, align_bytes=64)
        w2_scales = const.tile([P, E, K], U8, align_bytes=64)
        nc.vector.memset(w2_scales[:].bitcast(I32), 0)
        nc.sync.dma_start(
            out=w2_words[:].bitcast(I32),
            in_=ew2_words.rearrange("e p n t -> p e (n t)").bitcast(I32),
        )
        for quad in range(4):
            nc.sync.dma_start(
                out=w2_scales[32 * quad : 32 * quad + 4].bitcast(I32),
                in_=ew2_scales[:, 4 * quad : 4 * quad + 4, :].rearrange("e r n -> r e n").bitcast(I32),
            )

        ident = const.tile([P, P], BF16)
        make_identity(nc, ident[:])
        eps = const.tile([P, 1], F32)
        nc.vector.memset(eps[:], EPS)
        warm_sqrt = const.tile([P, 1], F32)
        nc.scalar.activation(out=warm_sqrt[:], in_=eps[:], func=ACT.Sqrt)

        bn_t = psum_o.tile([P, PACK, 4, E * G], BF16, tag="o")
        for t in range(PACK):
            nc.tensor.transpose(
                bn_t[:, t].rearrange("p i r -> p (i r)"), bn_rows[:, t:H:PACK], ident[:]
            )

        ew1_t = const.tile([P, E, PACK, P], BF16)

        def transpose_ew1(e):
            ew1_ps = psum_o.tile([P, PACK, P], BF16, name="ew1_ps", tag="o")
            for t in range(PACK):
                nc.tensor.transpose(ew1_ps[:, t, :], ew1_rows[:, e, t, :], ident[:])
            return ew1_ps

        le_t = const.tile([P, CHUNKS, TILES, P], BF16)

        def transpose_le(pair):
            le_ps = psum_o.tile([P, 2, TILES, P], BF16, name="le_ps", tag="o")
            for c in range(2):
                n = 2 * pair + c
                nc.tensor.transpose(le_ps[:, c, 0, :], le_full[:, 0, n, :], ident[:])
                nc.tensor.transpose(le_ps[:, c, 1, :], le_rest[:, n, :], ident[:])
                nc.tensor.transpose(le_ps[:, c, 2, :], le_full[:, 1, n, :], ident[:])
            return le_ps

        std = const.tile([P, PACK, E * G], F32)
        rstd = const.tile([P, PACK, E * G], F32)
        gain = const.tile([P, PACK, E * G], F32)
        mean_gain = const.tile([P, PACK, E * G], F32)
        shift = const.tile([P, PACK, E * G], F32)
        nc.scalar.activation(out=std[:], in_=bn_t[:, :, 0, :], func=ACT.Sqrt, bias=eps[:], scale=1.0)
        warm_sigmoid = const.tile([P, 1], F32)
        nc.scalar.activation(out=warm_sigmoid[:], in_=std[:, 0, 0:1], func=ACT.Sigmoid)

        le_ps_of = {0: transpose_le(0)}
        ew1_ps_of = {0: transpose_ew1(0), 1: transpose_ew1(1)}

        nc.vector.reciprocal(out=rstd[:], in_=std[:])
        nc.vector.tensor_copy(out=le_t[:, 0], in_=le_ps_of[0][:, 0])
        nc.vector.tensor_tensor(out=gain[:], in0=bn_t[:, :, 1, :], in1=rstd[:], op=ALU.mult)
        nc.vector.tensor_copy(out=ew1_t[:, 0], in_=ew1_ps_of[0][:])
        nc.vector.tensor_tensor(out=mean_gain[:], in0=bn_t[:, :, 2, :], in1=gain[:], op=ALU.mult)
        nc.vector.tensor_copy(out=ew1_t[:, 1], in_=ew1_ps_of[1][:])
        nc.vector.tensor_tensor(out=shift[:], in0=bn_t[:, :, 3, :], in1=mean_gain[:], op=ALU.subtract)
        nc.vector.tensor_copy(out=le_t[:, 1], in_=le_ps_of[0][:, 1])

        planes_of = {}
        words_of = {}
        scales_of = {}
        sums_of = {}
        sel_of = {}

        u_of = {}
        grouped_of = {}

        def first_matmul(step, t):
            n, e = divmod(step, E)
            u = psum_u.tile([P, COLS], F32, name="u", tag="u")
            nc.tensor.matmul(
                out=u[:],
                lhsT=ew1_t[:, e, t, :],
                rhs=le_t[:, n].rearrange("s j c -> s (j c)"),
                start=True,
                stop=True,
            )
            u_of[step, t] = u

        def batch_norm(step, t, i):
            n, e = divmod(step, E)
            row = G * e + n + CHUNKS * i
            cols = slice(GCOLS * i, GCOLS * (i + 1))
            if t < PACK - vector_planes(step):
                nc.scalar.activation(
                    out=planes_of[step][:, t, cols],
                    in_=u_of[step, t][:, cols],
                    func=ACT.Identity,
                    bias=shift[:, t, row : row + 1],
                    scale=gain[:, t, row : row + 1],
                )
            else:
                nc.vector.tensor_scalar(
                    out=planes_of[step][:, t, cols],
                    in0=u_of[step, t][:, cols],
                    scalar1=gain[:, t, row : row + 1],
                    scalar2=shift[:, t, row : row + 1],
                    op0=ALU.mult,
                    op1=ALU.add,
                )

        def new_planes(step):
            planes = work.tile([P, PACK, COLS], BF16, name="planes", tag="planes")
            planes_of[step] = planes

        def hidden_layer(step):
            new_planes(step)
            for t in range(PACK):
                first_matmul(step, t)
                for i in range(2):
                    batch_norm(step, t, i)

        def regroup(step, cols):
            if step not in grouped_of:
                grouped = work.tile([P, COLS, PACK], BF16, name="grouped", tag="grouped", align_bytes=64)
                grouped_of[step] = grouped
            nc.vector.tensor_scalar_max(
                out=grouped_of[step][:, cols, :].rearrange("p (c i) t -> p c t i", i=RUN),
                in0=planes_of[step][:, :, cols].rearrange("p t (c i) -> p c t i", i=RUN),
                scalar1=0.0,
            )

        def quantise(step, cols):
            if step not in words_of:
                words = work.tile([P, COLS], U32, name="words", tag="words", align_bytes=64)
                scales = work.tile([P, COLS], U8, name="scales", tag="scales", align_bytes=64)
                words_of[step] = words
                scales_of[step] = scales
            nc.vector.quantize_mx(
                out=words_of[step][:, cols].bitcast(FP8X4),
                scales=scales_of[step][:, cols],
                in_=grouped_of[step][:, cols, :].rearrange("p c t -> p (c t)"),
            )

        def second_matmul(step, tiles):
            e = step % E
            sums = psum_o.tile([P, len(tiles), K], F32, name="sums", tag="o")
            for place, j in enumerate(tiles):
                cols = slice(P * j, P * (j + 1))
                nc.tensor.matmul_mx(
                    out=sums[:, place, :],
                    lhsT=words_of[step][:, cols].bitcast(FP8X4),
                    lhsT_scale=scales_of[step][:, cols],
                    rhs=w2_words[:, e, :].bitcast(FP8X4),
                    rhs_scale=w2_scales[:, e, :],
                    start=True,
                    stop=True,
                )
            sums_of[step] = sums

        def store(dst, result, n):
            nc.sync.dma_start(out=dst[0:P, n:G:CHUNKS, :], in_=result[:, 0:TILES:2, :])
            for i in range(2):
                nc.sync.dma_start(
                    out=dst[P:B, n + CHUNKS * i, :], in_=result[REST * i : REST * (i + 1), 1, :]
                )

        def leave_psum(step):
            n, e = divmod(step, E)
            if e == 0:
                sel = work.tile([P, TILES, K], F32, name="sel", tag="sel")
                nc.scalar.activation(out=sel[:], in_=sums_of[step][:], func=ACT.Sigmoid)
                sel_of[step] = sel
            else:
                layer_bias = work.tile([P, TILES, K], F32, name="layer_bias", tag="layer_bias")
                nc.scalar.copy(out=layer_bias[:], in_=sums_of[step][:])
                store(out_1, layer_bias, n)

        def stretch(step):
            if step % E == 0:
                sel = sel_of[step]
                nc.vector.tensor_scalar(
                    out=sel[:], in0=sel[:], scalar1=1.2, scalar2=-0.1, op0=ALU.mult, op1=ALU.add
                )

        def clip(step):
            n, e = divmod(step, E)
            if e == 0:
                sel = sel_of[step]
                nc.vector.tensor_scalar(
                    out=sel[:], in0=sel[:], scalar1=0.0, scalar2=1.0, op0=ALU.max, op1=ALU.min
                )
                store(out_0, sel, n)

        def live(step):
            return 0 <= step < STEPS

        ALL = slice(0, COLS)
        TWO_TILES = slice(0, 2 * P)
        THIRD_TILE = slice(2 * P, COLS)
        LAST = STEPS - 1

        for r in range(LAST):
            if live(r - 1):
                regroup(r - 1, ALL)
            if live(r - 3):
                stretch(r - 3)
            if live(r - 4):
                clip(r - 4)
            hidden_layer(r)
            if r + 1 < CHUNKS // 2:
                le_ps_of[r + 1] = transpose_le(r + 1)
                nc.scalar.copy(out=le_t[:, 2 * r + 2 : 2 * r + 4], in_=le_ps_of[r + 1][:])
            if live(r - 2):
                second_matmul(r - 2, range(TILES))
                leave_psum(r - 2)
            if live(r - 1):
                quantise(r - 1, TWO_TILES)
                quantise(r - 1, THIRD_TILE)

        regroup(LAST - 1, ALL)
        stretch(LAST - 3)
        new_planes(LAST)
        for t in range(PACK):
            first_matmul(LAST, t)
        for t in range(PACK):
            batch_norm(LAST, t, 0)
        second_matmul(LAST - 2, range(TILES))
        quantise(LAST - 1, TWO_TILES)
        quantise(LAST - 1, THIRD_TILE)
        for t in range(PACK):
            batch_norm(LAST, t, 1)
        regroup(LAST, slice(0, GCOLS))
        clip(LAST - 3)
        leave_psum(LAST - 2)
        regroup(LAST, slice(GCOLS, COLS))
        second_matmul(LAST - 1, range(TILES))
        leave_psum(LAST - 1)
        quantise(LAST, slice(0, P))
        quantise(LAST, slice(P, COLS))
        n_last = LAST // E
        layer_bias = work.tile([P, TILES, K], F32, name="layer_bias", tag="layer_bias")
        second_matmul(LAST, [0])
        nc.scalar.copy(out=layer_bias[:, 0:1, :], in_=sums_of[LAST][:])
        nc.sync.dma_start(out=out_1[0:P, n_last, :], in_=layer_bias[:, 0, :])
        second_matmul(LAST, [1, 2])
        stretch(LAST - 1)
        nc.scalar.copy(out=layer_bias[:, 1:TILES, :], in_=sums_of[LAST][:])
        nc.sync.dma_start(out=out_1[0:P, n_last + CHUNKS, :], in_=layer_bias[:, 2, :])
        for i in range(2):
            nc.sync.dma_start(
                out=out_1[P:B, n_last + CHUNKS * i, :], in_=layer_bias[REST * i : REST * (i + 1), 1, :]
            )
        clip(LAST - 1)
